import numpy as np
import ml_dtypes


def mxq(x, axis, fmt="e4m3"):
    dtype, down = {"e4m3": (ml_dtypes.float8_e4m3fn, 7), "e5m2": (ml_dtypes.float8_e5m2, 14)}[fmt]
    v = np.moveaxis(np.asarray(x, np.float32).astype(ml_dtypes.bfloat16).astype(np.float64), axis, -1)
    blocks = v.reshape(v.shape[:-1] + (-1, 32))
    amax = np.abs(blocks).max(-1, keepdims=True)
    byte = np.maximum(np.where(amax > 0, np.frexp(amax)[1] - 1 + 127, 0) - down, 1)
    scale = np.exp2(byte - 127.0)
    codes = (blocks / scale).astype(np.float32).astype(dtype).astype(np.float64)
    return np.moveaxis((codes * scale).reshape(v.shape), -1, axis)


WIDE = False


def mx_kscale(k):
    if not WIDE:
        return np.ones(k)
    levels = np.array([10, -10, 5, -5, 0])
    if k % 512:
        return np.exp2(np.random.permutation(np.resize(levels, k // 32))).repeat(32)
    a = np.empty((k // 512, 16))
    for p in range(k // 512):
        a[p, :8] = np.random.permutation(np.resize(levels, 8))
        for g in range(8):
            far = levels[np.abs(levels - a[p, g]) >= 10]
            a[p, g + 8] = far[np.random.randint(len(far))]
    return np.exp2(a.ravel()).repeat(32)


BF16 = ml_dtypes.bfloat16


def bf(x):
    return np.asarray(x, np.float32).astype(BF16)


def f64(x):
    return np.asarray(x).astype(np.float64)


B, NP, H, W, EMB = 2, 128, 16, 24, 256
L = NP + H * W
C2 = EMB + EMB
BN_EPS = 1e-5


def setup_inputs():
    s = mx_kscale(C2)
    return {'T1': bf(np.random.standard_normal((B, L, EMB)) * s[:EMB]),
            'T2': bf(np.random.standard_normal((B, L, EMB)) * s[EMB:]),
            'Wf': bf(np.random.standard_normal((EMB, C2)) / np.sqrt(C2) / s[None, :]),
            'bn_g': bf(1.0 + 0.1 * np.random.standard_normal(EMB)),
            'bn_b': bf(0.3 * np.random.standard_normal(EMB))}


def reference(T1, T2, Wf, bn_g, bn_b):
    joint = np.concatenate([f64(T1).swapaxes(1, 2), f64(T2).swapaxes(1, 2)], axis=1)
    y = mxq(f64(Wf), 1, 'e4m3') @ mxq(joint, 1, 'e4m3')
    mu = y.mean(axis=(0, 2), keepdims=True)
    var = y.var(axis=(0, 2), keepdims=True)
    y = (y - mu) / np.sqrt(var + BN_EPS)
    y = y * f64(bn_g)[None, :, None] + f64(bn_b)[None, :, None]
    y = np.maximum(y, 0.0)
    return y.swapaxes(1, 2)

@@ -1,0 +1,246 @@
+from contextlib import ExitStack
+
+import concourse.mybir as mybir
+from concourse.masks import make_identity
+
+F32 = mybir.dt.float32
+BF16 = mybir.dt.bfloat16
+U32 = mybir.dt.uint32
+U8 = mybir.dt.uint8
+FP8X4 = mybir.dt.float8_e4m3fn_x4
+ACT = mybir.ActivationFunctionType
+ALU = mybir.AluOpType
+
+P = 128
+PACK = 4
+STREAMS = 2
+ROWS = 1024
+EMB = 256
+K = STREAMS * EMB
+O_TILES = EMB // P
+ROW_TILES = ROWS // P
+UNIT_TILES = 2
+UNITS = ROW_TILES // UNIT_TILES
+UNIT_ROWS = UNIT_TILES * P
+CHUNKS = 2
+CHUNK_UNITS = UNITS // CHUNKS
+CHUNK_TILES = ROW_TILES // CHUNKS
+PSUM_BANKS = 8
+LEAD = 2
+BN_EPS = 1e-5
+BN_STATS_DIM = 6
+
+FLOPS = 2 * ROWS * K * EMB
+
+
+def tile_iag_pb_s_kernel(tc, T1, T2, Wf, bn_g, bn_b, out):
+    nc = tc.nc
+    streams = [
+        T.flatten_outer_dims().rearrange("(p j) k -> p j k", j=ROW_TILES) for T in (T1, T2)
+    ]
+    out_rows = out.flatten_outer_dims().rearrange("(p j) o -> p j o", j=ROW_TILES)
+
+    with ExitStack() as ctx:
+        ctx.enter_context(tc.manual_schedule())
+        keep = ctx.enter_context(tc.tile_pool(name="keep", bufs=1))
+        banks = ctx.enter_context(tc.psum_pool(name="banks", bufs=PSUM_BANKS))
+
+        w_raw = keep.tile([P, O_TILES * K], BF16)
+        nc.sync.dma_start(
+            out=w_raw[:].rearrange("p (t k) -> p t k", t=O_TILES),
+            in_=Wf.rearrange("(t p) k -> p t k", p=P),
+        )
+        x_raw = []
+        for c in range(CHUNKS):
+            raw = keep.tile([P, STREAMS * CHUNK_TILES * EMB], BF16, name="x_raw%d" % c)
+            x_raw.append(raw)
+            for u in range(STREAMS):
+                nc.sync.dma_start(
+                    out=raw[:].rearrange("p (j u k) -> p u j k", u=STREAMS, j=CHUNK_TILES)[
+                        :, u, :, :
+                    ],
+                    in_=streams[u][:, c * CHUNK_TILES : (c + 1) * CHUNK_TILES, :],
+                )
+        gb_rows = keep.tile([P, P], BF16)
+        nc.vector.memset(gb_rows[:], 0.0)
+        nc.scalar.dma_start(out=gb_rows[0:O_TILES, :], in_=bn_g.rearrange("(t o) -> t o", o=P))
+        nc.scalar.dma_start(
+            out=gb_rows[O_TILES : 2 * O_TILES, :], in_=bn_b.rearrange("(t o) -> t o", o=P)
+        )
+
+        ident = keep.tile([P, P], F32)
+        make_identity(nc, ident[:])
+        eps = keep.tile([P, 1], F32)
+        nc.vector.memset(eps[:], BN_EPS)
+        table_warm = keep.tile([P, 1], F32)
+        nc.scalar.activation(out=table_warm[:], in_=eps[:], func=ACT.Abs_reciprocal_sqrt)
+
+        w_words = w_raw[:].bitcast(F32).rearrange("p (t w e) -> p t e w", t=O_TILES, e=2)
+        w_bank = banks.tile([P, O_TILES, STREAMS, P], F32, tag="bank")
+        for t in range(O_TILES):
+            for u in range(STREAMS):
+                nc.tensor.transpose(w_bank[:, t, u, :], w_words[:, t, u, :], ident[:])
+        w_grouped = keep.tile([P, EMB * PACK], BF16, align_bytes=64)
+        nc.scalar.copy(
+            out=w_grouped[:].bitcast(F32).rearrange("p (t o u) -> p t o u", t=O_TILES, u=STREAMS),
+            in_=w_bank[:].rearrange("p t u o -> p t o u"),
+        )
+        w_codes = keep.tile([P, EMB], U32, align_bytes=64)
+        w_scales = keep.tile([P, EMB], U8, align_bytes=64)
+        nc.vector.quantize_mx(
+            out=w_codes[:].bitcast(FP8X4), scales=w_scales[:], in_=w_grouped[:]
+        )
+
+        x_banks = {}
+        x_codes = {}
+        x_scales = {}
+
+        def transpose_rows(c):
+            x_words = x_raw[c][:].bitcast(F32).rearrange(
+                "p (n i w e) -> p e n i w", e=2, n=CHUNK_UNITS, i=UNIT_TILES
+            )
+            for n in range(CHUNK_UNITS):
+                x_banks[c * CHUNK_UNITS + n] = banks.tile(
+                    [P, UNIT_TILES, STREAMS, P], F32, tag="bank", name="x_bank%d%d" % (c, n)
+                )
+            for u in range(STREAMS):
+                for n in range(CHUNK_UNITS):
+                    for i in range(UNIT_TILES):
+                        nc.tensor.transpose(
+                            x_banks[c * CHUNK_UNITS + n][:, i, u, :], x_words[:, u, n, i, :], ident[:]
+                        )
+
+        x_grouped = {}
+
+        def group(unit):
+            x_grouped[unit] = keep.tile(
+                [P, UNIT_ROWS * PACK], BF16, align_bytes=64, name="x_grouped%d" % unit
+            )
+            nc.scalar.copy(
+                out=x_grouped[unit][:].bitcast(F32).rearrange(
+                    "p (i r u) -> p i r u", i=UNIT_TILES, u=STREAMS
+                ),
+                in_=x_banks[unit][:].rearrange("p i u r -> p i r u"),
+            )
+
+        def quantise(unit):
+            x_codes[unit] = keep.tile([P, UNIT_ROWS], U32, align_bytes=64, name="x_codes%d" % unit)
+            x_scales[unit] = keep.tile([P, UNIT_ROWS], U8, align_bytes=64, name="x_scales%d" % unit)
+            nc.vector.quantize_mx(
+                out=x_codes[unit][:].bitcast(FP8X4),
+                scales=x_scales[unit][:],
+                in_=x_grouped[unit][:],
+            )
+
+        stats = keep.tile([P, O_TILES, UNITS, BN_STATS_DIM], F32)
+        y = {}
+
+        def multiply(unit):
+            for t in range(O_TILES):
+                o_cols = slice(t * P, (t + 1) * P)
+                y[t, unit] = banks.tile([P, UNIT_ROWS], F32, tag="bank", name="y%d%d" % (t, unit))
+                nc.tensor.matmul_mx(
+                    out=y[t, unit][:],
+                    lhsT=w_codes[:, o_cols].bitcast(FP8X4),
+                    lhsT_scale=w_scales[:, o_cols],
+                    rhs=x_codes[unit][:].bitcast(FP8X4),
+                    rhs_scale=x_scales[unit][:],
+                    start=True,
+                    stop=True,
+                )
+
+        def sum_up(unit):
+            for t in range(O_TILES):
+                nc.vector.bn_stats(out=stats[:, t, unit, :], in_=y[t, unit][:])
+
+        gb_wide = keep.tile([P, P], F32)
+        nc.vector.tensor_copy(out=gb_wide[:], in_=gb_rows[:])
+        transpose_rows(0)
+        gb_bank = banks.tile([P, P], F32, tag="bank")
+        nc.tensor.transpose(gb_bank[:], gb_wide[:], ident[:])
+        for unit in range(CHUNK_UNITS):
+            group(unit)
+            quantise(unit)
+        gain_shift = keep.tile([P, 2 * O_TILES], F32)
+        nc.vector.tensor_copy(out=gain_shift[:], in_=gb_bank[:, 0 : 2 * O_TILES])
+        gain = gain_shift[:, 0:O_TILES]
+        shift_in = gain_shift[:, O_TILES : 2 * O_TILES]
+        neg_gain = keep.tile([P, O_TILES], F32)
+        nc.vector.tensor_scalar_mul(out=neg_gain[:], in0=gain, scalar1=-1.0)
+
+        transpose_rows(1)
+        for unit in range(CHUNK_UNITS):
+            multiply(unit)
+        for unit in range(CHUNK_UNITS):
+            group(CHUNK_UNITS + unit)
+            sum_up(unit)
+            quantise(CHUNK_UNITS + unit)
+        for unit in range(CHUNK_UNITS, UNITS):
+            multiply(unit)
+            sum_up(unit)
+
+        mean_var = keep.tile([P, O_TILES, 2], F32)
+        for t in range(O_TILES):
+            nc.vector.bn_aggr(
+                out=mean_var[:, t, :], in_=stats[:, t, :, :].rearrange("p n s -> p (n s)")
+            )
+        rstd = keep.tile([P, O_TILES], F32)
+        nc.scalar.activation(
+            out=rstd[:], in_=mean_var[:, :, 1], func=ACT.Abs_reciprocal_sqrt, bias=eps[:, 0:1]
+        )
+        neg_mean_gain = keep.tile([P, O_TILES], F32)
+        nc.vector.tensor_mul(out=neg_mean_gain[:], in0=mean_var[:, :, 0], in1=neg_gain[:])
+        scale = keep.tile([P, O_TILES], F32)
+        nc.vector.tensor_mul(out=scale[:], in0=rstd[:], in1=gain)
+        shift = keep.tile([P, O_TILES], F32)
+        for t in range(O_TILES):
+            nc.vector.tensor_scalar(
+                out=shift[:, t : t + 1],
+                in0=neg_mean_gain[:, t : t + 1],
+                scalar1=rstd[:, t : t + 1],
+                scalar2=shift_in[:, t : t + 1],
+                op0=ALU.mult,
+                op1=ALU.add,
+            )
+
+        z = {}
+
+        def normalise(unit):
+            for t in range(O_TILES):
+                z[t, unit] = keep.tile([P, UNIT_ROWS], F32, name="z%d%d" % (t, unit))
+            nc.scalar.activation(
+                out=z[0, unit][:],
+                in_=y[0, unit][:],
+                func=ACT.Identity,
+                scale=scale[:, 0:1],
+                bias=shift[:, 0:1],
+            )
+            nc.vector.tensor_scalar(
+                out=z[1, unit][:],
+                in0=y[1, unit][:],
+                scalar1=scale[:, 1:2],
+                scalar2=shift[:, 1:2],
+                op0=ALU.mult,
+                op1=ALU.add,
+            )
+
+        def finish(unit):
+            result = keep.tile([P, UNIT_TILES, EMB], F32, name="result%d" % unit)
+            for i in range(UNIT_TILES):
+                out_bank = banks.tile([P, EMB], F32, tag="bank", name="out_bank%d%d" % (unit, i))
+                for t in range(O_TILES):
+                    nc.tensor.transpose(
+                        out_bank[:, t * P : (t + 1) * P], z[t, unit][:, i * P : (i + 1) * P], ident[:]
+                    )
+                if i == 0:
+                    nc.scalar.activation(out=result[:, i, :], in_=out_bank[:], func=ACT.Relu)
+                else:
+                    nc.vector.tensor_scalar_max(out=result[:, i, :], in0=out_bank[:], scalar1=0.0)
+                nc.sync.dma_start(out=out_rows[:, unit * UNIT_TILES + i, :], in_=result[:, i, :])
+
+        for unit in range(LEAD):
+            normalise(unit)
+        for unit in range(UNITS):
+            if unit + LEAD < UNITS:
+                normalise(unit + LEAD)
+            finish(unit)

@@ -13,22 +13,19 @@ ALU = mybir.AluOpType
 
 P = 128
 PACK = 4
-STREAMS = 2
 ROWS = 1024
 EMB = 256
-K = STREAMS * EMB
+K = 2 * EMB
 O_TILES = EMB // P
 ROW_TILES = ROWS // P
 UNIT_TILES = 2
 UNITS = ROW_TILES // UNIT_TILES
 UNIT_ROWS = UNIT_TILES * P
-CHUNKS = 2
-CHUNK_UNITS = UNITS // CHUNKS
-CHUNK_TILES = ROW_TILES // CHUNKS
+CHUNK_UNITS = (1, 1, 2)
 PSUM_BANKS = 8
-LEAD = 2
 BN_EPS = 1e-5
-BN_STATS_DIM = 6
+BN_TUPLE = 3
+SCALAR_UNIT = 2
 
 FLOPS = 2 * ROWS * K * EMB
 
@@ -50,197 +47,256 @@ def tile_iag_pb_s_kernel(tc, T1, T2, Wf, bn_g, bn_b, out):
             out=w_raw[:].rearrange("p (t k) -> p t k", t=O_TILES),
             in_=Wf.rearrange("(t p) k -> p t k", p=P),
         )
-        x_raw = []
-        for c in range(CHUNKS):
-            raw = keep.tile([P, STREAMS * CHUNK_TILES * EMB], BF16, name="x_raw%d" % c)
-            x_raw.append(raw)
-            for u in range(STREAMS):
+        x_words = {}
+        tile0 = 0
+        for c, units in enumerate(CHUNK_UNITS):
+            tiles = units * UNIT_TILES
+            raw = keep.tile([P, tiles * K], BF16, name="x_raw%d" % c)
+            for u in range(2):
                 nc.sync.dma_start(
-                    out=raw[:].rearrange("p (j u k) -> p u j k", u=STREAMS, j=CHUNK_TILES)[
-                        :, u, :, :
-                    ],
-                    in_=streams[u][:, c * CHUNK_TILES : (c + 1) * CHUNK_TILES, :],
+                    out=raw[:].rearrange("p (j u k) -> p u j k", u=2, k=EMB)[:, u, :, :],
+                    in_=streams[u][:, tile0 : tile0 + tiles, :],
                 )
-        gb_rows = keep.tile([P, P], BF16)
-        nc.vector.memset(gb_rows[:], 0.0)
-        nc.scalar.dma_start(out=gb_rows[0:O_TILES, :], in_=bn_g.rearrange("(t o) -> t o", o=P))
-        nc.scalar.dma_start(
-            out=gb_rows[O_TILES : 2 * O_TILES, :], in_=bn_b.rearrange("(t o) -> t o", o=P)
-        )
+            words = raw[:].bitcast(F32).rearrange("p (j w e) -> p j e w", e=2, w=P)
+            for j in range(tiles):
+                x_words[tile0 + j] = words[:, j, :, :]
+            tile0 += tiles
 
         ident = keep.tile([P, P], F32)
         make_identity(nc, ident[:])
+        gb_rows = keep.tile([P, P], BF16)
+        nc.vector.memset(gb_rows[:], 0.0)
+        nc.sync.dma_start(out=gb_rows[0:O_TILES, :], in_=bn_g.rearrange("(t o) -> t o", o=P))
+        nc.sync.dma_start(
+            out=gb_rows[O_TILES : 2 * O_TILES, :], in_=bn_b.rearrange("(t o) -> t o", o=P)
+        )
         eps = keep.tile([P, 1], F32)
         nc.vector.memset(eps[:], BN_EPS)
         table_warm = keep.tile([P, 1], F32)
         nc.scalar.activation(out=table_warm[:], in_=eps[:], func=ACT.Abs_reciprocal_sqrt)
 
         w_words = w_raw[:].bitcast(F32).rearrange("p (t w e) -> p t e w", t=O_TILES, e=2)
-        w_bank = banks.tile([P, O_TILES, STREAMS, P], F32, tag="bank")
-        for t in range(O_TILES):
-            for u in range(STREAMS):
-                nc.tensor.transpose(w_bank[:, t, u, :], w_words[:, t, u, :], ident[:])
+        w_bank = banks.tile([P, O_TILES, 2, P], F32, tag="bank")
         w_grouped = keep.tile([P, EMB * PACK], BF16, align_bytes=64)
-        nc.scalar.copy(
-            out=w_grouped[:].bitcast(F32).rearrange("p (t o u) -> p t o u", t=O_TILES, u=STREAMS),
-            in_=w_bank[:].rearrange("p t u o -> p t o u"),
-        )
         w_codes = keep.tile([P, EMB], U32, align_bytes=64)
         w_scales = keep.tile([P, EMB], U8, align_bytes=64)
+        x_bank, x_grouped, x_codes, x_scales = {}, {}, {}, {}
+        y, z = {}, {}
+        stats = keep.tile([P, O_TILES, 2 * UNITS - 1, BN_TUPLE], F32)
+        scalar_stats = stats[:, :, 2 * UNITS - 2, :]
+        nc.vector.memset(scalar_stats[:, :, 0:1], float(UNIT_ROWS))
+        mean_var = keep.tile([P, O_TILES, 2], F32)
+        rstd = keep.tile([P, O_TILES], F32)
+        scale = keep.tile([P, O_TILES], F32)
+        shift = keep.tile([P, O_TILES], F32)
+        neg_mean_gain = keep.tile([P, O_TILES], F32)
+
+        def col(tile, t):
+            return tile[:, t : t + 1]
+
+        def transpose_unit(n):
+            x_bank[n] = banks.tile([P, UNIT_TILES, 2, P], F32, tag="bank", name="x_bank%d" % n)
+            for i in range(UNIT_TILES):
+                for e in range(2):
+                    nc.tensor.transpose(
+                        x_bank[n][:, i, e, :], x_words[n * UNIT_TILES + i][:, e, :], ident[:]
+                    )
+
+        def group(n):
+            x_grouped[n] = keep.tile(
+                [P, UNIT_ROWS * PACK], BF16, align_bytes=64, name="x_grouped%d" % n
+            )
+            nc.scalar.copy(
+                out=x_grouped[n][:].bitcast(F32).rearrange(
+                    "p (i r e) -> p i r e", i=UNIT_TILES, e=2
+                ),
+                in_=x_bank[n][:].rearrange("p i e r -> p i r e"),
+            )
+
+        def quantise(n):
+            x_codes[n] = keep.tile([P, UNIT_ROWS], U32, align_bytes=64, name="x_codes%d" % n)
+            x_scales[n] = keep.tile([P, UNIT_ROWS], U8, align_bytes=64, name="x_scales%d" % n)
+            nc.vector.quantize_mx(
+                out=x_codes[n][:].bitcast(FP8X4), scales=x_scales[n][:], in_=x_grouped[n][:]
+            )
+
+        def multiply(t, n):
+            o_cols = slice(t * P, (t + 1) * P)
+            y[t, n] = banks.tile([P, UNIT_ROWS], F32, tag="bank", name="y%d%d" % (t, n))
+            nc.tensor.matmul_mx(
+                out=y[t, n][:],
+                lhsT=w_codes[:, o_cols].bitcast(FP8X4),
+                lhsT_scale=w_scales[:, o_cols],
+                rhs=x_codes[n][:].bitcast(FP8X4),
+                rhs_scale=x_scales[n][:],
+                start=True,
+                stop=True,
+            )
+
+        def sum_up(t, n):
+            place = n - (n > SCALAR_UNIT)
+            nc.vector.bn_stats(
+                out=stats[:, t, 2 * place : 2 * place + 2, :].rearrange("p a b -> p (a b)"),
+                in_=y[t, n][:],
+            )
+
+        def scalar_mean(t):
+            dump = keep.tile([P, UNIT_ROWS], F32, name="dump_mean%d" % t)
+            nc.scalar.activation(
+                out=dump[:],
+                in_=y[t, SCALAR_UNIT][:],
+                func=ACT.Copy,
+                scale=1.0 / UNIT_ROWS,
+                accum_out=scalar_stats[:, t, 1:2],
+            )
+
+        def scalar_squares(t):
+            dump = keep.tile([P, UNIT_ROWS], F32, name="dump_squares%d" % t)
+            nc.scalar.activation(
+                out=dump[:],
+                in_=y[t, SCALAR_UNIT][:],
+                func=ACT.Square,
+                scale=-1.0,
+                bias=scalar_stats[:, t, 1:2],
+                accum_out=scalar_stats[:, t, 2:3],
+            )
+
+        for t in range(O_TILES):
+            for e in range(2):
+                nc.tensor.transpose(w_bank[:, t, e, :], w_words[:, t, e, :], ident[:])
+        nc.vector.tensor_copy(
+            out=w_grouped[:].bitcast(F32).rearrange("p (t o e) -> p t o e", t=O_TILES, e=2),
+            in_=w_bank[:].rearrange("p t e o -> p t o e"),
+        )
         nc.vector.quantize_mx(
             out=w_codes[:].bitcast(FP8X4), scales=w_scales[:], in_=w_grouped[:]
         )
 
-        x_banks = {}
-        x_codes = {}
-        x_scales = {}
-
-        def transpose_rows(c):
-            x_words = x_raw[c][:].bitcast(F32).rearrange(
-                "p (n i w e) -> p e n i w", e=2, n=CHUNK_UNITS, i=UNIT_TILES
-            )
-            for n in range(CHUNK_UNITS):
-                x_banks[c * CHUNK_UNITS + n] = banks.tile(
-                    [P, UNIT_TILES, STREAMS, P], F32, tag="bank", name="x_bank%d%d" % (c, n)
-                )
-            for u in range(STREAMS):
-                for n in range(CHUNK_UNITS):
-                    for i in range(UNIT_TILES):
-                        nc.tensor.transpose(
-                            x_banks[c * CHUNK_UNITS + n][:, i, u, :], x_words[:, u, n, i, :], ident[:]
-                        )
-
-        x_grouped = {}
-
-        def group(unit):
-            x_grouped[unit] = keep.tile(
-                [P, UNIT_ROWS * PACK], BF16, align_bytes=64, name="x_grouped%d" % unit
-            )
-            nc.scalar.copy(
-                out=x_grouped[unit][:].bitcast(F32).rearrange(
-                    "p (i r u) -> p i r u", i=UNIT_TILES, u=STREAMS
-                ),
-                in_=x_banks[unit][:].rearrange("p i u r -> p i r u"),
-            )
-
-        def quantise(unit):
-            x_codes[unit] = keep.tile([P, UNIT_ROWS], U32, align_bytes=64, name="x_codes%d" % unit)
-            x_scales[unit] = keep.tile([P, UNIT_ROWS], U8, align_bytes=64, name="x_scales%d" % unit)
-            nc.vector.quantize_mx(
-                out=x_codes[unit][:].bitcast(FP8X4),
-                scales=x_scales[unit][:],
-                in_=x_grouped[unit][:],
-            )
-
-        stats = keep.tile([P, O_TILES, UNITS, BN_STATS_DIM], F32)
-        y = {}
-
-        def multiply(unit):
-            for t in range(O_TILES):
-                o_cols = slice(t * P, (t + 1) * P)
-                y[t, unit] = banks.tile([P, UNIT_ROWS], F32, tag="bank", name="y%d%d" % (t, unit))
-                nc.tensor.matmul_mx(
-                    out=y[t, unit][:],
-                    lhsT=w_codes[:, o_cols].bitcast(FP8X4),
-                    lhsT_scale=w_scales[:, o_cols],
-                    rhs=x_codes[unit][:].bitcast(FP8X4),
-                    rhs_scale=x_scales[unit][:],
-                    start=True,
-                    stop=True,
-                )
-
-        def sum_up(unit):
-            for t in range(O_TILES):
-                nc.vector.bn_stats(out=stats[:, t, unit, :], in_=y[t, unit][:])
-
+        transpose_unit(0)
+        group(0)
+        quantise(0)
+        transpose_unit(1)
+        group(1)
+        quantise(1)
+        transpose_unit(2)
+        group(2)
+        quantise(2)
+        transpose_unit(3)
+        group(3)
         gb_wide = keep.tile([P, P], F32)
         nc.vector.tensor_copy(out=gb_wide[:], in_=gb_rows[:])
-        transpose_rows(0)
         gb_bank = banks.tile([P, P], F32, tag="bank")
         nc.tensor.transpose(gb_bank[:], gb_wide[:], ident[:])
-        for unit in range(CHUNK_UNITS):
-            group(unit)
-            quantise(unit)
         gain_shift = keep.tile([P, 2 * O_TILES], F32)
-        nc.vector.tensor_copy(out=gain_shift[:], in_=gb_bank[:, 0 : 2 * O_TILES])
+        nc.scalar.copy(out=gain_shift[:], in_=gb_bank[:, 0 : 2 * O_TILES])
         gain = gain_shift[:, 0:O_TILES]
         shift_in = gain_shift[:, O_TILES : 2 * O_TILES]
         neg_gain = keep.tile([P, O_TILES], F32)
-        nc.vector.tensor_scalar_mul(out=neg_gain[:], in0=gain, scalar1=-1.0)
-
-        transpose_rows(1)
-        for unit in range(CHUNK_UNITS):
-            multiply(unit)
-        for unit in range(CHUNK_UNITS):
-            group(CHUNK_UNITS + unit)
-            sum_up(unit)
-            quantise(CHUNK_UNITS + unit)
-        for unit in range(CHUNK_UNITS, UNITS):
-            multiply(unit)
-            sum_up(unit)
-
-        mean_var = keep.tile([P, O_TILES, 2], F32)
-        for t in range(O_TILES):
-            nc.vector.bn_aggr(
-                out=mean_var[:, t, :], in_=stats[:, t, :, :].rearrange("p n s -> p (n s)")
-            )
-        rstd = keep.tile([P, O_TILES], F32)
         nc.scalar.activation(
-            out=rstd[:], in_=mean_var[:, :, 1], func=ACT.Abs_reciprocal_sqrt, bias=eps[:, 0:1]
+            out=neg_gain[:], in_=gb_bank[:, 0:O_TILES], func=ACT.Copy, scale=-1.0
         )
-        neg_mean_gain = keep.tile([P, O_TILES], F32)
-        nc.vector.tensor_mul(out=neg_mean_gain[:], in0=mean_var[:, :, 0], in1=neg_gain[:])
-        scale = keep.tile([P, O_TILES], F32)
-        nc.vector.tensor_mul(out=scale[:], in0=rstd[:], in1=gain)
-        shift = keep.tile([P, O_TILES], F32)
-        for t in range(O_TILES):
-            nc.vector.tensor_scalar(
-                out=shift[:, t : t + 1],
-                in0=neg_mean_gain[:, t : t + 1],
-                scalar1=rstd[:, t : t + 1],
-                scalar2=shift_in[:, t : t + 1],
-                op0=ALU.mult,
-                op1=ALU.add,
+        multiply(0, 0)
+        multiply(0, 1)
+        multiply(0, 2)
+        multiply(1, 2)
+        sum_up(0, 0)
+        quantise(3)
+        sum_up(0, 1)
+        multiply(1, 0)
+        multiply(1, 1)
+        multiply(0, 3)
+        multiply(1, 3)
+        scalar_mean(0)
+        scalar_mean(1)
+        scalar_squares(0)
+        scalar_squares(1)
+        sum_up(0, 3)
+        sum_up(1, 0)
+
+        def aggregate(t):
+            nc.vector.bn_aggr(
+                out=mean_var[:, t, :], in_=stats[:, t, :, :].rearrange("p a b -> p (a b)")
             )
 
-        z = {}
-
-        def normalise(unit):
-            for t in range(O_TILES):
-                z[t, unit] = keep.tile([P, UNIT_ROWS], F32, name="z%d%d" % (t, unit))
+        def root(t):
             nc.scalar.activation(
-                out=z[0, unit][:],
-                in_=y[0, unit][:],
-                func=ACT.Identity,
-                scale=scale[:, 0:1],
-                bias=shift[:, 0:1],
+                out=col(rstd, t),
+                in_=mean_var[:, t, 1:2],
+                func=ACT.Abs_reciprocal_sqrt,
+                bias=eps[:, 0:1],
             )
+
+        def make_scale(t):
+            nc.vector.tensor_mul(out=col(scale, t), in0=col(rstd, t), in1=col(gain, t))
+
+        def center(t):
+            nc.vector.tensor_mul(
+                out=col(neg_mean_gain, t), in0=mean_var[:, t, 0:1], in1=col(neg_gain, t)
+            )
+
+        def make_shift(t):
             nc.vector.tensor_scalar(
-                out=z[1, unit][:],
-                in0=y[1, unit][:],
-                scalar1=scale[:, 1:2],
-                scalar2=shift[:, 1:2],
+                out=col(shift, t),
+                in0=col(neg_mean_gain, t),
+                scalar1=col(rstd, t),
+                scalar2=col(shift_in, t),
                 op0=ALU.mult,
                 op1=ALU.add,
             )
 
-        def finish(unit):
-            result = keep.tile([P, UNIT_TILES, EMB], F32, name="result%d" % unit)
+        def normalise_on_vector(t, n):
+            z[t, n] = keep.tile([P, UNIT_ROWS], F32, name="z%d%d" % (t, n))
+            nc.vector.tensor_scalar(
+                out=z[t, n][:],
+                in0=y[t, n][:],
+                scalar1=col(scale, t),
+                scalar2=col(shift, t),
+                op0=ALU.mult,
+                op1=ALU.add,
+            )
+
+        def normalise_on_scalar(t, n):
+            z[t, n] = keep.tile([P, UNIT_ROWS], F32, name="z%d%d" % (t, n))
+            nc.scalar.activation(
+                out=z[t, n][:],
+                in_=y[t, n][:],
+                func=ACT.Identity,
+                scale=col(scale, t),
+                bias=col(shift, t),
+            )
+
+        aggregate(0)
+        root(0)
+        sum_up(1, 1)
+        center(0)
+        make_scale(0)
+        make_shift(0)
+        sum_up(1, 3)
+        aggregate(1)
+        normalise_on_scalar(0, 0)
+        root(1)
+        normalise_on_scalar(0, 1)
+        center(1)
+        make_scale(1)
+        make_shift(1)
+        normalise_on_vector(1, 0)
+        normalise_on_vector(1, 1)
+
+        for n in range(UNITS):
+            if n + 2 < UNITS:
+                normalise_on_scalar(0, n + 2)
+                normalise_on_vector(1, n + 2)
+            result = keep.tile([P, UNIT_TILES, EMB], F32, name="result%d" % n)
             for i in range(UNIT_TILES):
-                out_bank = banks.tile([P, EMB], F32, tag="bank", name="out_bank%d%d" % (unit, i))
+                out_bank = banks.tile([P, EMB], F32, tag="bank", name="out_bank%d%d" % (n, i))
                 for t in range(O_TILES):
                     nc.tensor.transpose(
-                        out_bank[:, t * P : (t + 1) * P], z[t, unit][:, i * P : (i + 1) * P], ident[:]
+                        out_bank[:, t * P : (t + 1) * P],
+                        z[t, n][:, i * P : (i + 1) * P],
+                        ident[:],
                     )
                 if i == 0:
                     nc.scalar.activation(out=result[:, i, :], in_=out_bank[:], func=ACT.Relu)
                 else:
                     nc.vector.tensor_scalar_max(out=result[:, i, :], in0=out_bank[:], scalar1=0.0)
-                nc.sync.dma_start(out=out_rows[:, unit * UNIT_TILES + i, :], in_=result[:, i, :])
-
-        for unit in range(LEAD):
-            normalise(unit)
-        for unit in range(UNITS):
-            if unit + LEAD < UNITS:
-                normalise(unit + LEAD)
-            finish(unit)
+                nc.sync.dma_start(out=out_rows[:, n * UNIT_TILES + i, :], in_=result[:, i, :])

@@ -21,11 +21,13 @@ ROW_TILES = ROWS // P
 UNIT_TILES = 2
 UNITS = ROW_TILES // UNIT_TILES
 UNIT_ROWS = UNIT_TILES * P
-CHUNK_UNITS = (1, 1, 2)
+CHUNK_UNITS = (1, 1, 1, 1)
 PSUM_BANKS = 8
+FIRST_IDLE_COLS = 384
+LATER_IDLE_COLS = 208
 BN_EPS = 1e-5
 BN_TUPLE = 3
-SCALAR_UNIT = 2
+SCALAR_UNIT = 1
 
 FLOPS = 2 * ROWS * K * EMB
 
@@ -61,15 +63,22 @@ def tile_iag_pb_s_kernel(tc, T1, T2, Wf, bn_g, bn_b, out):
             for j in range(tiles):
                 x_words[tile0 + j] = words[:, j, :, :]
             tile0 += tiles
+        gain_raw = keep.tile([P, O_TILES, 2], BF16)
+        shift_raw = keep.tile([P, O_TILES, 2], BF16)
+        with nc.allow_non_contiguous_dma(reason="256 values, one channel a partition"):
+            nc.sync.dma_start(out=gain_raw[:, :, 0], in_=bn_g.rearrange("(t p) -> p t", p=P))
+            nc.sync.dma_start(out=shift_raw[:, :, 0], in_=bn_b.rearrange("(t p) -> p t", p=P))
 
+        idle_operand = keep.tile([P, FIRST_IDLE_COLS], F32)
+        nc.vector.memset(idle_operand[:], 0.0)
+        idle_bank = banks.tile([P, FIRST_IDLE_COLS], F32, tag="bank")
+
+        def keep_awake(out, moving):
+            nc.tensor.matmul(out, lhsT=idle_operand[:, 0:P], rhs=moving, start=True, stop=True)
+
+        keep_awake(idle_bank[:], idle_operand[:])
         ident = keep.tile([P, P], F32)
         make_identity(nc, ident[:])
-        gb_rows = keep.tile([P, P], BF16)
-        nc.vector.memset(gb_rows[:], 0.0)
-        nc.sync.dma_start(out=gb_rows[0:O_TILES, :], in_=bn_g.rearrange("(t o) -> t o", o=P))
-        nc.sync.dma_start(
-            out=gb_rows[O_TILES : 2 * O_TILES, :], in_=bn_b.rearrange("(t o) -> t o", o=P)
-        )
         eps = keep.tile([P, 1], F32)
         nc.vector.memset(eps[:], BN_EPS)
         table_warm = keep.tile([P, 1], F32)
@@ -81,15 +90,17 @@ def tile_iag_pb_s_kernel(tc, T1, T2, Wf, bn_g, bn_b, out):
         w_codes = keep.tile([P, EMB], U32, align_bytes=64)
         w_scales = keep.tile([P, EMB], U8, align_bytes=64)
         x_bank, x_grouped, x_codes, x_scales = {}, {}, {}, {}
-        y, z = {}, {}
+        y, y_bank, z = {}, {}, {}
         stats = keep.tile([P, O_TILES, 2 * UNITS - 1, BN_TUPLE], F32)
         scalar_stats = stats[:, :, 2 * UNITS - 2, :]
         nc.vector.memset(scalar_stats[:, :, 0:1], float(UNIT_ROWS))
         mean_var = keep.tile([P, O_TILES, 2], F32)
         rstd = keep.tile([P, O_TILES], F32)
-        scale = keep.tile([P, O_TILES], F32)
-        shift = keep.tile([P, O_TILES], F32)
-        neg_mean_gain = keep.tile([P, O_TILES], F32)
+        factors = keep.tile([P, O_TILES, 2], F32)
+        addends = keep.tile([P, O_TILES, 2], F32)
+        scale_shift = keep.tile([P, O_TILES, 2], F32)
+        nc.gpsimd.memset(addends[:, :, 0], 0.0)
+        neg_gain = keep.tile([P, O_TILES], F32)
 
         def col(tile, t):
             return tile[:, t : t + 1]
@@ -122,9 +133,12 @@ def tile_iag_pb_s_kernel(tc, T1, T2, Wf, bn_g, bn_b, out):
 
         def multiply(t, n):
             o_cols = slice(t * P, (t + 1) * P)
-            y[t, n] = banks.tile([P, UNIT_ROWS], F32, tag="bank", name="y%d%d" % (t, n))
+            y_bank[t, n] = banks.tile(
+                [P, UNIT_ROWS + LATER_IDLE_COLS], F32, tag="bank", name="y%d%d" % (t, n)
+            )
+            y[t, n] = y_bank[t, n][:, 0:UNIT_ROWS]
             nc.tensor.matmul_mx(
-                out=y[t, n][:],
+                out=y[t, n],
                 lhsT=w_codes[:, o_cols].bitcast(FP8X4),
                 lhsT_scale=w_scales[:, o_cols],
                 rhs=x_codes[n][:].bitcast(FP8X4),
@@ -137,14 +151,14 @@ def tile_iag_pb_s_kernel(tc, T1, T2, Wf, bn_g, bn_b, out):
             place = n - (n > SCALAR_UNIT)
             nc.vector.bn_stats(
                 out=stats[:, t, 2 * place : 2 * place + 2, :].rearrange("p a b -> p (a b)"),
-                in_=y[t, n][:],
+                in_=y[t, n],
             )
 
         def scalar_mean(t):
             dump = keep.tile([P, UNIT_ROWS], F32, name="dump_mean%d" % t)
             nc.scalar.activation(
                 out=dump[:],
-                in_=y[t, SCALAR_UNIT][:],
+                in_=y[t, SCALAR_UNIT],
                 func=ACT.Copy,
                 scale=1.0 / UNIT_ROWS,
                 accum_out=scalar_stats[:, t, 1:2],
@@ -154,7 +168,7 @@ def tile_iag_pb_s_kernel(tc, T1, T2, Wf, bn_g, bn_b, out):
             dump = keep.tile([P, UNIT_ROWS], F32, name="dump_squares%d" % t)
             nc.scalar.activation(
                 out=dump[:],
-                in_=y[t, SCALAR_UNIT][:],
+                in_=y[t, SCALAR_UNIT],
                 func=ACT.Square,
                 scale=-1.0,
                 bias=scalar_stats[:, t, 1:2],
@@ -183,35 +197,29 @@ def tile_iag_pb_s_kernel(tc, T1, T2, Wf, bn_g, bn_b, out):
         quantise(2)
         transpose_unit(3)
         group(3)
-        gb_wide = keep.tile([P, P], F32)
-        nc.vector.tensor_copy(out=gb_wide[:], in_=gb_rows[:])
-        gb_bank = banks.tile([P, P], F32, tag="bank")
-        nc.tensor.transpose(gb_bank[:], gb_wide[:], ident[:])
-        gain_shift = keep.tile([P, 2 * O_TILES], F32)
-        nc.scalar.copy(out=gain_shift[:], in_=gb_bank[:, 0 : 2 * O_TILES])
-        gain = gain_shift[:, 0:O_TILES]
-        shift_in = gain_shift[:, O_TILES : 2 * O_TILES]
-        neg_gain = keep.tile([P, O_TILES], F32)
-        nc.scalar.activation(
-            out=neg_gain[:], in_=gb_bank[:, 0:O_TILES], func=ACT.Copy, scale=-1.0
-        )
+        nc.gpsimd.tensor_copy(out=factors[:, :, 0], in_=gain_raw[:, :, 0])
+        nc.gpsimd.tensor_copy(out=addends[:, :, 1], in_=shift_raw[:, :, 0])
+        nc.gpsimd.tensor_scalar_mul(out=neg_gain[:], in0=gain_raw[:, :, 0], scalar1=-1.0)
         multiply(0, 0)
+        multiply(1, 0)
         multiply(0, 1)
-        multiply(0, 2)
-        multiply(1, 2)
+        multiply(1, 1)
         sum_up(0, 0)
         quantise(3)
-        sum_up(0, 1)
-        multiply(1, 0)
-        multiply(1, 1)
-        multiply(0, 3)
-        multiply(1, 3)
-        scalar_mean(0)
-        scalar_mean(1)
-        scalar_squares(0)
-        scalar_squares(1)
-        sum_up(0, 3)
         sum_up(1, 0)
+        for t in range(O_TILES):
+            multiply(t, 2)
+        for t in range(O_TILES):
+            multiply(t, 3)
+        for t in range(O_TILES):
+            keep_awake(y_bank[t, 0][:, UNIT_ROWS:], idle_operand[:, 0:LATER_IDLE_COLS])
+        for t in range(O_TILES):
+            scalar_mean(t)
+        for t in range(O_TILES):
+            scalar_squares(t)
+        sum_up(0, 2)
+        sum_up(0, 3)
+        sum_up(1, 2)
 
         def aggregate(t):
             nc.vector.bn_aggr(
@@ -226,20 +234,17 @@ def tile_iag_pb_s_kernel(tc, T1, T2, Wf, bn_g, bn_b, out):
                 bias=eps[:, 0:1],
             )
 
-        def make_scale(t):
-            nc.vector.tensor_mul(out=col(scale, t), in0=col(rstd, t), in1=col(gain, t))
-
         def center(t):
             nc.vector.tensor_mul(
-                out=col(neg_mean_gain, t), in0=mean_var[:, t, 0:1], in1=col(neg_gain, t)
+                out=factors[:, t, 1:2], in0=mean_var[:, t, 0:1], in1=col(neg_gain, t)
             )
 
-        def make_shift(t):
-            nc.vector.tensor_scalar(
-                out=col(shift, t),
-                in0=col(neg_mean_gain, t),
-                scalar1=col(rstd, t),
-                scalar2=col(shift_in, t),
+        def make_scale_shift(t):
+            nc.vector.scalar_tensor_tensor(
+                out=scale_shift[:, t, :],
+                in0=factors[:, t, :],
+                scalar=col(rstd, t),
+                in1=addends[:, t, :],
                 op0=ALU.mult,
                 op1=ALU.add,
             )
@@ -248,9 +253,9 @@ def tile_iag_pb_s_kernel(tc, T1, T2, Wf, bn_g, bn_b, out):
             z[t, n] = keep.tile([P, UNIT_ROWS], F32, name="z%d%d" % (t, n))
             nc.vector.tensor_scalar(
                 out=z[t, n][:],
-                in0=y[t, n][:],
-                scalar1=col(scale, t),
-                scalar2=col(shift, t),
+                in0=y[t, n],
+                scalar1=scale_shift[:, t, 0:1],
+                scalar2=scale_shift[:, t, 1:2],
                 op0=ALU.mult,
                 op1=ALU.add,
             )
@@ -259,27 +264,24 @@ def tile_iag_pb_s_kernel(tc, T1, T2, Wf, bn_g, bn_b, out):
             z[t, n] = keep.tile([P, UNIT_ROWS], F32, name="z%d%d" % (t, n))
             nc.scalar.activation(
                 out=z[t, n][:],
-                in_=y[t, n][:],
+                in_=y[t, n],
                 func=ACT.Identity,
-                scale=col(scale, t),
-                bias=col(shift, t),
+                scale=scale_shift[:, t, 0:1],
+                bias=scale_shift[:, t, 1:2],
             )
 
         aggregate(0)
         root(0)
-        sum_up(1, 1)
-        center(0)
-        make_scale(0)
-        make_shift(0)
         sum_up(1, 3)
+        center(0)
         aggregate(1)
-        normalise_on_scalar(0, 0)
         root(1)
-        normalise_on_scalar(0, 1)
+        make_scale_shift(0)
         center(1)
-        make_scale(1)
-        make_shift(1)
+        make_scale_shift(1)
+        normalise_on_scalar(0, 0)
         normalise_on_vector(1, 0)
+        normalise_on_scalar(0, 1)
         normalise_on_vector(1, 1)
 
         for n in range(UNITS):

@@ -23,8 +23,9 @@ UNITS = ROW_TILES // UNIT_TILES
 UNIT_ROWS = UNIT_TILES * P
 CHUNK_UNITS = (1, 1, 1, 1)
 PSUM_BANKS = 8
-FIRST_IDLE_COLS = 384
+FIRST_IDLE_COLS = 352
 LATER_IDLE_COLS = 208
+LAST_IDLE_COLS = 256
 BN_EPS = 1e-5
 BN_TUPLE = 3
 SCALAR_UNIT = 1
@@ -77,6 +78,8 @@ def tile_iag_pb_s_kernel(tc, T1, T2, Wf, bn_g, bn_b, out):
             nc.tensor.matmul(out, lhsT=idle_operand[:, 0:P], rhs=moving, start=True, stop=True)
 
         keep_awake(idle_bank[:], idle_operand[:])
+        late_operand = keep.tile([P, LAST_IDLE_COLS], F32)
+        nc.gpsimd.memset(late_operand[:], 0.0)
         ident = keep.tile([P, P], F32)
         make_identity(nc, ident[:])
         eps = keep.tile([P, 1], F32)
@@ -134,7 +137,7 @@ def tile_iag_pb_s_kernel(tc, T1, T2, Wf, bn_g, bn_b, out):
         def multiply(t, n):
             o_cols = slice(t * P, (t + 1) * P)
             y_bank[t, n] = banks.tile(
-                [P, UNIT_ROWS + LATER_IDLE_COLS], F32, tag="bank", name="y%d%d" % (t, n)
+                [P, UNIT_ROWS + LAST_IDLE_COLS], F32, tag="bank", name="y%d%d" % (t, n)
             )
             y[t, n] = y_bank[t, n][:, 0:UNIT_ROWS]
             nc.tensor.matmul_mx(
@@ -211,8 +214,7 @@ def tile_iag_pb_s_kernel(tc, T1, T2, Wf, bn_g, bn_b, out):
             multiply(t, 2)
         for t in range(O_TILES):
             multiply(t, 3)
-        for t in range(O_TILES):
-            keep_awake(y_bank[t, 0][:, UNIT_ROWS:], idle_operand[:, 0:LATER_IDLE_COLS])
+        keep_awake(y_bank[0, 0][:, UNIT_ROWS : UNIT_ROWS + LATER_IDLE_COLS], idle_operand[:, 0:LATER_IDLE_COLS])
         for t in range(O_TILES):
             scalar_mean(t)
         for t in range(O_TILES):
@@ -235,7 +237,7 @@ def tile_iag_pb_s_kernel(tc, T1, T2, Wf, bn_g, bn_b, out):
             )
 
         def center(t):
-            nc.vector.tensor_mul(
+            nc.gpsimd.tensor_mul(
                 out=factors[:, t, 1:2], in0=mean_var[:, t, 0:1], in1=col(neg_gain, t)
             )
 
@@ -249,22 +251,24 @@ def tile_iag_pb_s_kernel(tc, T1, T2, Wf, bn_g, bn_b, out):
                 op1=ALU.add,
             )
 
-        def normalise_on_vector(t, n):
-            z[t, n] = keep.tile([P, UNIT_ROWS], F32, name="z%d%d" % (t, n))
+        for n in range(UNITS):
+            for t in range(O_TILES):
+                z[t, n] = keep.tile([P, UNIT_ROWS], F32, name="z%d%d" % (t, n))
+
+        def normalise_on_vector(t, n, rows):
             nc.vector.tensor_scalar(
-                out=z[t, n][:],
-                in0=y[t, n],
+                out=z[t, n][:, rows],
+                in0=y[t, n][:, rows],
                 scalar1=scale_shift[:, t, 0:1],
                 scalar2=scale_shift[:, t, 1:2],
                 op0=ALU.mult,
                 op1=ALU.add,
             )
 
-        def normalise_on_scalar(t, n):
-            z[t, n] = keep.tile([P, UNIT_ROWS], F32, name="z%d%d" % (t, n))
+        def normalise_on_scalar(t, n, rows):
             nc.scalar.activation(
-                out=z[t, n][:],
-                in_=y[t, n],
+                out=z[t, n][:, rows],
+                in_=y[t, n][:, rows],
                 func=ACT.Identity,
                 scale=scale_shift[:, t, 0:1],
                 bias=scale_shift[:, t, 1:2],
@@ -272,22 +276,24 @@ def tile_iag_pb_s_kernel(tc, T1, T2, Wf, bn_g, bn_b, out):
 
         aggregate(0)
         root(0)
-        sum_up(1, 3)
         center(0)
+        nc.gpsimd.tensor_copy(out=late_operand[:, 0:1], in_=mean_var[:, 0, 0:1])
+        keep_awake(y_bank[1, 0][:, UNIT_ROWS:], late_operand[:])
+        sum_up(1, 3)
         aggregate(1)
         root(1)
-        make_scale_shift(0)
         center(1)
+        make_scale_shift(0)
         make_scale_shift(1)
-        normalise_on_scalar(0, 0)
-        normalise_on_vector(1, 0)
-        normalise_on_scalar(0, 1)
-        normalise_on_vector(1, 1)
+        for n in range(UNITS):
+            parts = UNIT_TILES if n == 0 else 1
+            width = UNIT_ROWS // parts
+            for part in range(parts):
+                rows = slice(part * width, (part + 1) * width)
+                normalise_on_vector(0, n, rows)
+                normalise_on_scalar(1, n, rows)
 
         for n in range(UNITS):
-            if n + 2 < UNITS:
-                normalise_on_scalar(0, n + 2)
-                normalise_on_vector(1, n + 2)
             result = keep.tile([P, UNIT_TILES, EMB], F32, name="result%d" % n)
             for i in range(UNIT_TILES):
                 out_bank = banks.tile([P, EMB], F32, tag="bank", name="out_bank%d%d" % (n, i))

@@ -23,9 +23,8 @@ UNITS = ROW_TILES // UNIT_TILES
 UNIT_ROWS = UNIT_TILES * P
 CHUNK_UNITS = (1, 1, 1, 1)
 PSUM_BANKS = 8
-FIRST_IDLE_COLS = 352
+FIRST_IDLE_COLS = 384
 LATER_IDLE_COLS = 208
-LAST_IDLE_COLS = 256
 BN_EPS = 1e-5
 BN_TUPLE = 3
 SCALAR_UNIT = 1
@@ -78,8 +77,6 @@ def tile_iag_pb_s_kernel(tc, T1, T2, Wf, bn_g, bn_b, out):
             nc.tensor.matmul(out, lhsT=idle_operand[:, 0:P], rhs=moving, start=True, stop=True)
 
         keep_awake(idle_bank[:], idle_operand[:])
-        late_operand = keep.tile([P, LAST_IDLE_COLS], F32)
-        nc.gpsimd.memset(late_operand[:], 0.0)
         ident = keep.tile([P, P], F32)
         make_identity(nc, ident[:])
         eps = keep.tile([P, 1], F32)
@@ -137,7 +134,7 @@ def tile_iag_pb_s_kernel(tc, T1, T2, Wf, bn_g, bn_b, out):
         def multiply(t, n):
             o_cols = slice(t * P, (t + 1) * P)
             y_bank[t, n] = banks.tile(
-                [P, UNIT_ROWS + LAST_IDLE_COLS], F32, tag="bank", name="y%d%d" % (t, n)
+                [P, UNIT_ROWS + LATER_IDLE_COLS], F32, tag="bank", name="y%d%d" % (t, n)
             )
             y[t, n] = y_bank[t, n][:, 0:UNIT_ROWS]
             nc.tensor.matmul_mx(
@@ -214,7 +211,8 @@ def tile_iag_pb_s_kernel(tc, T1, T2, Wf, bn_g, bn_b, out):
             multiply(t, 2)
         for t in range(O_TILES):
             multiply(t, 3)
-        keep_awake(y_bank[0, 0][:, UNIT_ROWS : UNIT_ROWS + LATER_IDLE_COLS], idle_operand[:, 0:LATER_IDLE_COLS])
+        for t in range(O_TILES):
+            keep_awake(y_bank[t, 0][:, UNIT_ROWS:], idle_operand[:, 0:LATER_IDLE_COLS])
         for t in range(O_TILES):
             scalar_mean(t)
         for t in range(O_TILES):
@@ -237,8 +235,11 @@ def tile_iag_pb_s_kernel(tc, T1, T2, Wf, bn_g, bn_b, out):
             )
 
         def center(t):
-            nc.gpsimd.tensor_mul(
-                out=factors[:, t, 1:2], in0=mean_var[:, t, 0:1], in1=col(neg_gain, t)
+            nc.scalar.activation(
+                out=factors[:, t, 1:2],
+                in_=mean_var[:, t, 0:1],
+                func=ACT.Copy,
+                scale=col(neg_gain, t),
             )
 
         def make_scale_shift(t):
@@ -275,14 +276,12 @@ def tile_iag_pb_s_kernel(tc, T1, T2, Wf, bn_g, bn_b, out):
             )
 
         aggregate(0)
-        root(0)
         center(0)
-        nc.gpsimd.tensor_copy(out=late_operand[:, 0:1], in_=mean_var[:, 0, 0:1])
-        keep_awake(y_bank[1, 0][:, UNIT_ROWS:], late_operand[:])
+        root(0)
         sum_up(1, 3)
         aggregate(1)
-        root(1)
         center(1)
+        root(1)
         make_scale_shift(0)
         make_scale_shift(1)
         for n in range(UNITS):

@@ -23,11 +23,12 @@ UNITS = ROW_TILES // UNIT_TILES
 UNIT_ROWS = UNIT_TILES * P
 CHUNK_UNITS = (1, 1, 1, 1)
 PSUM_BANKS = 8
+LEAD = 2
 FIRST_IDLE_COLS = 384
 LATER_IDLE_COLS = 208
 BN_EPS = 1e-5
 BN_TUPLE = 3
-SCALAR_UNIT = 1
+SCALAR_SUMS = ((0, 1), (1, 1), (1, 0))
 
 FLOPS = 2 * ROWS * K * EMB
 
@@ -91,9 +92,17 @@ def tile_iag_pb_s_kernel(tc, T1, T2, Wf, bn_g, bn_b, out):
         w_scales = keep.tile([P, EMB], U8, align_bytes=64)
         x_bank, x_grouped, x_codes, x_scales = {}, {}, {}, {}
         y, y_bank, z = {}, {}, {}
-        stats = keep.tile([P, O_TILES, 2 * UNITS - 1, BN_TUPLE], F32)
-        scalar_stats = stats[:, :, 2 * UNITS - 2, :]
-        nc.vector.memset(scalar_stats[:, :, 0:1], float(UNIT_ROWS))
+        stats, triple = {}, {}
+        for t in range(O_TILES):
+            on_scalar = [n for n in range(UNITS) if (t, n) in SCALAR_SUMS]
+            on_vector = [n for n in range(UNITS) if (t, n) not in SCALAR_SUMS]
+            count = len(on_scalar) + 2 * len(on_vector)
+            stats[t] = keep.tile([P, count, BN_TUPLE], F32, name="stats%d" % t)
+            nc.vector.memset(stats[t][:, 0 : len(on_scalar), 0:1], float(UNIT_ROWS))
+            for place, n in enumerate(on_scalar):
+                triple[t, n] = place
+            for place, n in enumerate(on_vector):
+                triple[t, n] = len(on_scalar) + 2 * place
         mean_var = keep.tile([P, O_TILES, 2], F32)
         rstd = keep.tile([P, O_TILES], F32)
         factors = keep.tile([P, O_TILES, 2], F32)
@@ -105,23 +114,25 @@ def tile_iag_pb_s_kernel(tc, T1, T2, Wf, bn_g, bn_b, out):
         def col(tile, t):
             return tile[:, t : t + 1]
 
-        def transpose_unit(n):
-            x_bank[n] = banks.tile([P, UNIT_TILES, 2, P], F32, tag="bank", name="x_bank%d" % n)
-            for i in range(UNIT_TILES):
+        def transpose_tiles(n, tiles):
+            bank = banks.tile([P, len(tiles), 2, P], F32, tag="bank", name="x_bank%d%d" % (n, tiles[0]))
+            for place, i in enumerate(tiles):
                 for e in range(2):
                     nc.tensor.transpose(
-                        x_bank[n][:, i, e, :], x_words[n * UNIT_TILES + i][:, e, :], ident[:]
+                        bank[:, place, e, :], x_words[n * UNIT_TILES + i][:, e, :], ident[:]
                     )
+            x_bank[n, tiles] = bank
 
-        def group(n):
-            x_grouped[n] = keep.tile(
-                [P, UNIT_ROWS * PACK], BF16, align_bytes=64, name="x_grouped%d" % n
-            )
+        def group(n, tiles):
+            if n not in x_grouped:
+                x_grouped[n] = keep.tile(
+                    [P, UNIT_ROWS * PACK], BF16, align_bytes=64, name="x_grouped%d" % n
+                )
             nc.scalar.copy(
                 out=x_grouped[n][:].bitcast(F32).rearrange(
                     "p (i r e) -> p i r e", i=UNIT_TILES, e=2
-                ),
-                in_=x_bank[n][:].rearrange("p i e r -> p i r e"),
+                )[:, tiles[0] : tiles[-1] + 1, :, :],
+                in_=x_bank[n, tiles][:].rearrange("p i e r -> p i r e"),
             )
 
         def quantise(n):
@@ -148,31 +159,30 @@ def tile_iag_pb_s_kernel(tc, T1, T2, Wf, bn_g, bn_b, out):
             )
 
         def sum_up(t, n):
-            place = n - (n > SCALAR_UNIT)
+            place = triple[t, n]
             nc.vector.bn_stats(
-                out=stats[:, t, 2 * place : 2 * place + 2, :].rearrange("p a b -> p (a b)"),
-                in_=y[t, n],
+                out=stats[t][:, place : place + 2, :].rearrange("p a b -> p (a b)"), in_=y[t, n]
             )
 
-        def scalar_mean(t):
-            dump = keep.tile([P, UNIT_ROWS], F32, name="dump_mean%d" % t)
+        def scalar_mean(t, n):
+            dump = keep.tile([P, UNIT_ROWS], F32, name="dump_mean%d%d" % (t, n))
             nc.scalar.activation(
                 out=dump[:],
-                in_=y[t, SCALAR_UNIT],
+                in_=y[t, n],
                 func=ACT.Copy,
                 scale=1.0 / UNIT_ROWS,
-                accum_out=scalar_stats[:, t, 1:2],
+                accum_out=stats[t][:, triple[t, n], 1:2],
             )
 
-        def scalar_squares(t):
-            dump = keep.tile([P, UNIT_ROWS], F32, name="dump_squares%d" % t)
+        def scalar_squares(t, n):
+            dump = keep.tile([P, UNIT_ROWS], F32, name="dump_squares%d%d" % (t, n))
             nc.scalar.activation(
                 out=dump[:],
-                in_=y[t, SCALAR_UNIT],
+                in_=y[t, n],
                 func=ACT.Square,
                 scale=-1.0,
-                bias=scalar_stats[:, t, 1:2],
-                accum_out=scalar_stats[:, t, 2:3],
+                bias=stats[t][:, triple[t, n], 1:2],
+                accum_out=stats[t][:, triple[t, n], 2:3],
             )
 
         for t in range(O_TILES):
@@ -186,44 +196,36 @@ def tile_iag_pb_s_kernel(tc, T1, T2, Wf, bn_g, bn_b, out):
             out=w_codes[:].bitcast(FP8X4), scales=w_scales[:], in_=w_grouped[:]
         )
 
-        transpose_unit(0)
-        group(0)
-        quantise(0)
-        transpose_unit(1)
-        group(1)
-        quantise(1)
-        transpose_unit(2)
-        group(2)
-        quantise(2)
-        transpose_unit(3)
-        group(3)
+        whole = tuple(range(UNIT_TILES))
+        for n in range(UNITS - 1):
+            transpose_tiles(n, whole)
+            group(n, whole)
+            quantise(n)
+        for i in range(UNIT_TILES):
+            transpose_tiles(UNITS - 1, (i,))
+            group(UNITS - 1, (i,))
+        quantise(UNITS - 1)
         nc.gpsimd.tensor_copy(out=factors[:, :, 0], in_=gain_raw[:, :, 0])
         nc.gpsimd.tensor_copy(out=addends[:, :, 1], in_=shift_raw[:, :, 0])
         nc.gpsimd.tensor_scalar_mul(out=neg_gain[:], in0=gain_raw[:, :, 0], scalar1=-1.0)
-        multiply(0, 0)
-        multiply(1, 0)
-        multiply(0, 1)
-        multiply(1, 1)
+        for t, n in ((0, 1), (1, 1), (1, 0), (0, 0), (0, 2), (1, 2), (0, 3), (1, 3)):
+            multiply(t, n)
+        scalar_mean(0, 1)
+        scalar_mean(1, 1)
+        scalar_squares(0, 1)
+        scalar_mean(1, 0)
+        scalar_squares(1, 1)
+        scalar_squares(1, 0)
         sum_up(0, 0)
-        quantise(3)
-        sum_up(1, 0)
-        for t in range(O_TILES):
-            multiply(t, 2)
-        for t in range(O_TILES):
-            multiply(t, 3)
-        for t in range(O_TILES):
-            keep_awake(y_bank[t, 0][:, UNIT_ROWS:], idle_operand[:, 0:LATER_IDLE_COLS])
-        for t in range(O_TILES):
-            scalar_mean(t)
-        for t in range(O_TILES):
-            scalar_squares(t)
+        for n in range(2):
+            keep_awake(y_bank[0, n][:, UNIT_ROWS:], idle_operand[:, 0:LATER_IDLE_COLS])
         sum_up(0, 2)
         sum_up(0, 3)
         sum_up(1, 2)
 
         def aggregate(t):
             nc.vector.bn_aggr(
-                out=mean_var[:, t, :], in_=stats[:, t, :, :].rearrange("p a b -> p (a b)")
+                out=mean_var[:, t, :], in_=stats[t][:].rearrange("p a b -> p (a b)")
             )
 
         def root(t):
@@ -284,7 +286,7 @@ def tile_iag_pb_s_kernel(tc, T1, T2, Wf, bn_g, bn_b, out):
         root(1)
         make_scale_shift(0)
         make_scale_shift(1)
-        for n in range(UNITS):
+        def normalise(n):
             parts = UNIT_TILES if n == 0 else 1
             width = UNIT_ROWS // parts
             for part in range(parts):
@@ -292,7 +294,12 @@ def tile_iag_pb_s_kernel(tc, T1, T2, Wf, bn_g, bn_b, out):
                 normalise_on_vector(0, n, rows)
                 normalise_on_scalar(1, n, rows)
 
+        for n in range(LEAD):
+            normalise(n)
+
         for n in range(UNITS):
+            if n + LEAD < UNITS:
+                normalise(n + LEAD)
             result = keep.tile([P, UNIT_TILES, EMB], F32, name="result%d" % n)
             for i in range(UNIT_TILES):
                 out_bank = banks.tile([P, EMB], F32, tag="bank", name="out_bank%d%d" % (n, i))

@@ -47,8 +47,7 @@ def tile_iag_pb_s_kernel(tc, T1, T2, Wf, bn_g, bn_b, out):
 
         w_raw = keep.tile([P, O_TILES * K], BF16)
         nc.sync.dma_start(
-            out=w_raw[:].rearrange("p (t k) -> p t k", t=O_TILES),
-            in_=Wf.rearrange("(t p) k -> p t k", p=P),
+            out=w_raw[:], in_=Wf.rearrange("(p t) k -> p (t k)", t=O_TILES)
         )
         x_words = {}
         tile0 = 0
@@ -64,11 +63,10 @@ def tile_iag_pb_s_kernel(tc, T1, T2, Wf, bn_g, bn_b, out):
             for j in range(tiles):
                 x_words[tile0 + j] = words[:, j, :, :]
             tile0 += tiles
-        gain_raw = keep.tile([P, O_TILES, 2], BF16)
-        shift_raw = keep.tile([P, O_TILES, 2], BF16)
-        with nc.allow_non_contiguous_dma(reason="256 values, one channel a partition"):
-            nc.sync.dma_start(out=gain_raw[:, :, 0], in_=bn_g.rearrange("(t p) -> p t", p=P))
-            nc.sync.dma_start(out=shift_raw[:, :, 0], in_=bn_b.rearrange("(t p) -> p t", p=P))
+        gain_raw = keep.tile([P, O_TILES], BF16)
+        shift_raw = keep.tile([P, O_TILES], BF16)
+        nc.sync.dma_start(out=gain_raw[:], in_=bn_g.rearrange("(p t) -> p t", t=O_TILES))
+        nc.sync.dma_start(out=shift_raw[:], in_=bn_b.rearrange("(p t) -> p t", t=O_TILES))
 
         idle_operand = keep.tile([P, FIRST_IDLE_COLS], F32)
         nc.vector.memset(idle_operand[:], 0.0)
@@ -205,9 +203,9 @@ def tile_iag_pb_s_kernel(tc, T1, T2, Wf, bn_g, bn_b, out):
             transpose_tiles(UNITS - 1, (i,))
             group(UNITS - 1, (i,))
         quantise(UNITS - 1)
-        nc.gpsimd.tensor_copy(out=factors[:, :, 0], in_=gain_raw[:, :, 0])
-        nc.gpsimd.tensor_copy(out=addends[:, :, 1], in_=shift_raw[:, :, 0])
-        nc.gpsimd.tensor_scalar_mul(out=neg_gain[:], in0=gain_raw[:, :, 0], scalar1=-1.0)
+        nc.gpsimd.tensor_copy(out=factors[:, :, 0], in_=gain_raw[:])
+        nc.gpsimd.tensor_copy(out=addends[:, :, 1], in_=shift_raw[:])
+        nc.gpsimd.tensor_scalar_mul(out=neg_gain[:], in0=gain_raw[:], scalar1=-1.0)
         for t, n in ((0, 1), (1, 1), (1, 0), (0, 0), (0, 2), (1, 2), (0, 3), (1, 3)):
             multiply(t, n)
         scalar_mean(0, 1)
@@ -309,8 +307,15 @@ def tile_iag_pb_s_kernel(tc, T1, T2, Wf, bn_g, bn_b, out):
                         z[t, n][:, i * P : (i + 1) * P],
                         ident[:],
                     )
+                source = out_bank[:].rearrange("p (t o) -> p o t", t=O_TILES)
+                target = result[:, i, :].rearrange("p (o t) -> p o t", t=O_TILES)
                 if i == 0:
-                    nc.scalar.activation(out=result[:, i, :], in_=out_bank[:], func=ACT.Relu)
+                    nc.scalar.activation(out=target, in_=source, func=ACT.Relu)
                 else:
-                    nc.vector.tensor_scalar_max(out=result[:, i, :], in0=out_bank[:], scalar1=0.0)
-                nc.sync.dma_start(out=out_rows[:, n * UNIT_TILES + i, :], in_=result[:, i, :])
+                    nc.vector.tensor_scalar_max(out=target, in0=source, scalar1=0.0)
+                if n == 0:
+                    nc.sync.dma_start(out=out_rows[:, i, :], in_=result[:, i, :])
+            if n > 0:
+                nc.sync.dma_start(
+                    out=out_rows[:, n * UNIT_TILES : (n + 1) * UNIT_TILES, :], in_=result[:]
+                )

@@ -22,13 +22,14 @@ UNIT_TILES = 2
 UNITS = ROW_TILES // UNIT_TILES
 UNIT_ROWS = UNIT_TILES * P
 CHUNK_UNITS = (1, 1, 1, 1)
+UNITS_BEFORE_W = 1
 PSUM_BANKS = 8
 LEAD = 2
-FIRST_IDLE_COLS = 384
-LATER_IDLE_COLS = 208
+FIRST_IDLE_COLS = 304
+LATER_IDLE_COLS = 256
 BN_EPS = 1e-5
 BN_TUPLE = 3
-SCALAR_SUMS = ((0, 1), (1, 1), (1, 0))
+SCALAR_SUMS = ((0, 0), (1, 0), (1, 1))
 
 FLOPS = 2 * ROWS * K * EMB
 
@@ -46,13 +47,14 @@ def tile_iag_pb_s_kernel(tc, T1, T2, Wf, bn_g, bn_b, out):
         banks = ctx.enter_context(tc.psum_pool(name="banks", bufs=PSUM_BANKS))
 
         w_raw = keep.tile([P, O_TILES * K], BF16)
-        nc.sync.dma_start(
-            out=w_raw[:], in_=Wf.rearrange("(p t) k -> p (t k)", t=O_TILES)
-        )
         x_words = {}
         tile0 = 0
         for c, units in enumerate(CHUNK_UNITS):
             tiles = units * UNIT_TILES
+            if c == UNITS_BEFORE_W:
+                nc.sync.dma_start(
+                    out=w_raw[:], in_=Wf.rearrange("(p t) k -> p (t k)", t=O_TILES)
+                )
             raw = keep.tile([P, tiles * K], BF16, name="x_raw%d" % c)
             for u in range(2):
                 nc.sync.dma_start(
@@ -183,6 +185,10 @@ def tile_iag_pb_s_kernel(tc, T1, T2, Wf, bn_g, bn_b, out):
                 accum_out=stats[t][:, triple[t, n], 2:3],
             )
 
+        whole = tuple(range(UNIT_TILES))
+        for n in range(UNITS_BEFORE_W):
+            transpose_tiles(n, whole)
+            group(n, whole)
         for t in range(O_TILES):
             for e in range(2):
                 nc.tensor.transpose(w_bank[:, t, e, :], w_words[:, t, e, :], ident[:])
@@ -193,9 +199,8 @@ def tile_iag_pb_s_kernel(tc, T1, T2, Wf, bn_g, bn_b, out):
         nc.vector.quantize_mx(
             out=w_codes[:].bitcast(FP8X4), scales=w_scales[:], in_=w_grouped[:]
         )
-
-        whole = tuple(range(UNIT_TILES))
-        for n in range(UNITS - 1):
+        quantise(0)
+        for n in range(UNITS_BEFORE_W, UNITS - 1):
             transpose_tiles(n, whole)
             group(n, whole)
             quantise(n)
@@ -206,17 +211,16 @@ def tile_iag_pb_s_kernel(tc, T1, T2, Wf, bn_g, bn_b, out):
         nc.gpsimd.tensor_copy(out=factors[:, :, 0], in_=gain_raw[:])
         nc.gpsimd.tensor_copy(out=addends[:, :, 1], in_=shift_raw[:])
         nc.gpsimd.tensor_scalar_mul(out=neg_gain[:], in0=gain_raw[:], scalar1=-1.0)
-        for t, n in ((0, 1), (1, 1), (1, 0), (0, 0), (0, 2), (1, 2), (0, 3), (1, 3)):
+        for t, n in ((0, 0), (1, 0), (1, 1), (0, 1), (0, 2), (1, 2), (0, 3), (1, 3)):
             multiply(t, n)
-        scalar_mean(0, 1)
-        scalar_mean(1, 1)
-        scalar_squares(0, 1)
+        scalar_mean(0, 0)
         scalar_mean(1, 0)
-        scalar_squares(1, 1)
+        scalar_squares(0, 0)
+        scalar_mean(1, 1)
         scalar_squares(1, 0)
-        sum_up(0, 0)
-        for n in range(2):
-            keep_awake(y_bank[0, n][:, UNIT_ROWS:], idle_operand[:, 0:LATER_IDLE_COLS])
+        scalar_squares(1, 1)
+        sum_up(0, 1)
+        keep_awake(y_bank[0, 1][:, UNIT_ROWS:], idle_operand[:, 0:LATER_IDLE_COLS])
         sum_up(0, 2)
         sum_up(0, 3)
         sum_up(1, 2)
@@ -279,6 +283,7 @@ def tile_iag_pb_s_kernel(tc, T1, T2, Wf, bn_g, bn_b, out):
         center(0)
         root(0)
         sum_up(1, 3)
+        keep_awake(y_bank[1, 3][:, UNIT_ROWS:], idle_operand[:, 0:LATER_IDLE_COLS])
         aggregate(1)
         center(1)
         root(1)

from contextlib import ExitStack

import concourse.mybir as mybir
from concourse.masks import make_identity

F32 = mybir.dt.float32
BF16 = mybir.dt.bfloat16
U32 = mybir.dt.uint32
U8 = mybir.dt.uint8
FP8X4 = mybir.dt.float8_e4m3fn_x4
ACT = mybir.ActivationFunctionType
ALU = mybir.AluOpType

P = 128
PACK = 4
ROWS = 1024
EMB = 256
K = 2 * EMB
O_TILES = EMB // P
ROW_TILES = ROWS // P
UNIT_TILES = 2
UNITS = ROW_TILES // UNIT_TILES
UNIT_ROWS = UNIT_TILES * P
CHUNK_UNITS = (1, 1, 1, 1)
UNITS_BEFORE_W = 1
PSUM_BANKS = 8
LEAD = 2
FIRST_IDLE_COLS = 304
LATER_IDLE_COLS = 256
BN_EPS = 1e-5
BN_TUPLE = 3
SCALAR_SUMS = ((0, 0), (1, 0), (1, 1))

FLOPS = 2 * ROWS * K * EMB


def tile_iag_pb_s_kernel(tc, T1, T2, Wf, bn_g, bn_b, out):
    nc = tc.nc
    streams = [
        T.flatten_outer_dims().rearrange("(p j) k -> p j k", j=ROW_TILES) for T in (T1, T2)
    ]
    out_rows = out.flatten_outer_dims().rearrange("(p j) o -> p j o", j=ROW_TILES)

    with ExitStack() as ctx:
        ctx.enter_context(tc.manual_schedule())
        keep = ctx.enter_context(tc.tile_pool(name="keep", bufs=1))
        banks = ctx.enter_context(tc.psum_pool(name="banks", bufs=PSUM_BANKS))

        w_raw = keep.tile([P, O_TILES * K], BF16)
        x_words = {}
        tile0 = 0
        for c, units in enumerate(CHUNK_UNITS):
            tiles = units * UNIT_TILES
            if c == UNITS_BEFORE_W:
                nc.sync.dma_start(
                    out=w_raw[:], in_=Wf.rearrange("(p t) k -> p (t k)", t=O_TILES)
                )
            raw = keep.tile([P, tiles * K], BF16, name="x_raw%d" % c)
            for u in range(2):
                nc.sync.dma_start(
                    out=raw[:].rearrange("p (j u k) -> p u j k", u=2, k=EMB)[:, u, :, :],
                    in_=streams[u][:, tile0 : tile0 + tiles, :],
                )
            words = raw[:].bitcast(F32).rearrange("p (j w e) -> p j e w", e=2, w=P)
            for j in range(tiles):
                x_words[tile0 + j] = words[:, j, :, :]
            tile0 += tiles
        gain_raw = keep.tile([P, O_TILES], BF16)
        shift_raw = keep.tile([P, O_TILES], BF16)
        nc.sync.dma_start(out=gain_raw[:], in_=bn_g.rearrange("(p t) -> p t", t=O_TILES))
        nc.sync.dma_start(out=shift_raw[:], in_=bn_b.rearrange("(p t) -> p t", t=O_TILES))

        idle_operand = keep.tile([P, FIRST_IDLE_COLS], F32)
        nc.vector.memset(idle_operand[:], 0.0)
        idle_bank = banks.tile([P, FIRST_IDLE_COLS], F32, tag="bank")

        def keep_awake(out, moving):
            nc.tensor.matmul(out, lhsT=idle_operand[:, 0:P], rhs=moving, start=True, stop=True)

        keep_awake(idle_bank[:], idle_operand[:])
        ident = keep.tile([P, P], F32)
        make_identity(nc, ident[:])
        eps = keep.tile([P, 1], F32)
        nc.vector.memset(eps[:], BN_EPS)
        table_warm = keep.tile([P, 1], F32)
        nc.scalar.activation(out=table_warm[:], in_=eps[:], func=ACT.Abs_reciprocal_sqrt)

        w_words = w_raw[:].bitcast(F32).rearrange("p (t w e) -> p t e w", t=O_TILES, e=2)
        w_bank = banks.tile([P, O_TILES, 2, P], F32, tag="bank")
        w_grouped = keep.tile([P, EMB * PACK], BF16, align_bytes=64)
        w_codes = keep.tile([P, EMB], U32, align_bytes=64)
        w_scales = keep.tile([P, EMB], U8, align_bytes=64)
        x_bank, x_grouped, x_codes, x_scales = {}, {}, {}, {}
        y, y_bank, z = {}, {}, {}
        stats, triple = {}, {}
        for t in range(O_TILES):
            on_scalar = [n for n in range(UNITS) if (t, n) in SCALAR_SUMS]
            on_vector = [n for n in range(UNITS) if (t, n) not in SCALAR_SUMS]
            count = len(on_scalar) + 2 * len(on_vector)
            stats[t] = keep.tile([P, count, BN_TUPLE], F32, name="stats%d" % t)
            nc.vector.memset(stats[t][:, 0 : len(on_scalar), 0:1], float(UNIT_ROWS))
            for place, n in enumerate(on_scalar):
                triple[t, n] = place
            for place, n in enumerate(on_vector):
                triple[t, n] = len(on_scalar) + 2 * place
        mean_var = keep.tile([P, O_TILES, 2], F32)
        rstd = keep.tile([P, O_TILES], F32)
        factors = keep.tile([P, O_TILES, 2], F32)
        addends = keep.tile([P, O_TILES, 2], F32)
        scale_shift = keep.tile([P, O_TILES, 2], F32)
        nc.gpsimd.memset(addends[:, :, 0], 0.0)
        neg_gain = keep.tile([P, O_TILES], F32)

        def col(tile, t):
            return tile[:, t : t + 1]

        def transpose_tiles(n, tiles):
            bank = banks.tile([P, len(tiles), 2, P], F32, tag="bank", name="x_bank%d%d" % (n, tiles[0]))
            for place, i in enumerate(tiles):
                for e in range(2):
                    nc.tensor.transpose(
                        bank[:, place, e, :], x_words[n * UNIT_TILES + i][:, e, :], ident[:]
                    )
            x_bank[n, tiles] = bank

        def group(n, tiles):
            if n not in x_grouped:
                x_grouped[n] = keep.tile(
                    [P, UNIT_ROWS * PACK], BF16, align_bytes=64, name="x_grouped%d" % n
                )
            nc.scalar.copy(
                out=x_grouped[n][:].bitcast(F32).rearrange(
                    "p (i r e) -> p i r e", i=UNIT_TILES, e=2
                )[:, tiles[0] : tiles[-1] + 1, :, :],
                in_=x_bank[n, tiles][:].rearrange("p i e r -> p i r e"),
            )

        def quantise(n):
            x_codes[n] = keep.tile([P, UNIT_ROWS], U32, align_bytes=64, name="x_codes%d" % n)
            x_scales[n] = keep.tile([P, UNIT_ROWS], U8, align_bytes=64, name="x_scales%d" % n)
            nc.vector.quantize_mx(
                out=x_codes[n][:].bitcast(FP8X4), scales=x_scales[n][:], in_=x_grouped[n][:]
            )

        def multiply(t, n):
            o_cols = slice(t * P, (t + 1) * P)
            y_bank[t, n] = banks.tile(
                [P, UNIT_ROWS + LATER_IDLE_COLS], F32, tag="bank", name="y%d%d" % (t, n)
            )
            y[t, n] = y_bank[t, n][:, 0:UNIT_ROWS]
            nc.tensor.matmul_mx(
                out=y[t, n],
                lhsT=w_codes[:, o_cols].bitcast(FP8X4),
                lhsT_scale=w_scales[:, o_cols],
                rhs=x_codes[n][:].bitcast(FP8X4),
                rhs_scale=x_scales[n][:],
                start=True,
                stop=True,
            )

        def sum_up(t, n):
            place = triple[t, n]
            nc.vector.bn_stats(
                out=stats[t][:, place : place + 2, :].rearrange("p a b -> p (a b)"), in_=y[t, n]
            )

        def scalar_mean(t, n):
            dump = keep.tile([P, UNIT_ROWS], F32, name="dump_mean%d%d" % (t, n))
            nc.scalar.activation(
                out=dump[:],
                in_=y[t, n],
                func=ACT.Copy,
                scale=1.0 / UNIT_ROWS,
                accum_out=stats[t][:, triple[t, n], 1:2],
            )

        def scalar_squares(t, n):
            dump = keep.tile([P, UNIT_ROWS], F32, name="dump_squares%d%d" % (t, n))
            nc.scalar.activation(
                out=dump[:],
                in_=y[t, n],
                func=ACT.Square,
                scale=-1.0,
                bias=stats[t][:, triple[t, n], 1:2],
                accum_out=stats[t][:, triple[t, n], 2:3],
            )

        whole = tuple(range(UNIT_TILES))
        for n in range(UNITS_BEFORE_W):
            transpose_tiles(n, whole)
            group(n, whole)
        for t in range(O_TILES):
            for e in range(2):
                nc.tensor.transpose(w_bank[:, t, e, :], w_words[:, t, e, :], ident[:])
        nc.vector.tensor_copy(
            out=w_grouped[:].bitcast(F32).rearrange("p (t o e) -> p t o e", t=O_TILES, e=2),
            in_=w_bank[:].rearrange("p t e o -> p t o e"),
        )
        nc.vector.quantize_mx(
            out=w_codes[:].bitcast(FP8X4), scales=w_scales[:], in_=w_grouped[:]
        )
        quantise(0)
        for n in range(UNITS_BEFORE_W, UNITS - 1):
            transpose_tiles(n, whole)
            group(n, whole)
            quantise(n)
        for i in range(UNIT_TILES):
            transpose_tiles(UNITS - 1, (i,))
            group(UNITS - 1, (i,))
        quantise(UNITS - 1)
        nc.gpsimd.tensor_copy(out=factors[:, :, 0], in_=gain_raw[:])
        nc.gpsimd.tensor_copy(out=addends[:, :, 1], in_=shift_raw[:])
        nc.gpsimd.tensor_scalar_mul(out=neg_gain[:], in0=gain_raw[:], scalar1=-1.0)
        for t, n in ((0, 0), (1, 0), (1, 1), (0, 1), (0, 2), (1, 2), (0, 3), (1, 3)):
            multiply(t, n)
        scalar_mean(0, 0)
        scalar_mean(1, 0)
        scalar_squares(0, 0)
        scalar_mean(1, 1)
        scalar_squares(1, 0)
        scalar_squares(1, 1)
        sum_up(0, 1)
        keep_awake(y_bank[0, 1][:, UNIT_ROWS:], idle_operand[:, 0:LATER_IDLE_COLS])
        sum_up(0, 2)
        sum_up(0, 3)
        sum_up(1, 2)

        def aggregate(t):
            nc.vector.bn_aggr(
                out=mean_var[:, t, :], in_=stats[t][:].rearrange("p a b -> p (a b)")
            )

        def root(t):
            nc.scalar.activation(
                out=col(rstd, t),
                in_=mean_var[:, t, 1:2],
                func=ACT.Abs_reciprocal_sqrt,
                bias=eps[:, 0:1],
            )

        def center(t):
            nc.scalar.activation(
                out=factors[:, t, 1:2],
                in_=mean_var[:, t, 0:1],
                func=ACT.Copy,
                scale=col(neg_gain, t),
            )

        def make_scale_shift(t):
            nc.vector.scalar_tensor_tensor(
                out=scale_shift[:, t, :],
                in0=factors[:, t, :],
                scalar=col(rstd, t),
                in1=addends[:, t, :],
                op0=ALU.mult,
                op1=ALU.add,
            )

        for n in range(UNITS):
            for t in range(O_TILES):
                z[t, n] = keep.tile([P, UNIT_ROWS], F32, name="z%d%d" % (t, n))

        def normalise_on_vector(t, n, rows):
            nc.vector.tensor_scalar(
                out=z[t, n][:, rows],
                in0=y[t, n][:, rows],
                scalar1=scale_shift[:, t, 0:1],
                scalar2=scale_shift[:, t, 1:2],
                op0=ALU.mult,
                op1=ALU.add,
            )

        def normalise_on_scalar(t, n, rows):
            nc.scalar.activation(
                out=z[t, n][:, rows],
                in_=y[t, n][:, rows],
                func=ACT.Identity,
                scale=scale_shift[:, t, 0:1],
                bias=scale_shift[:, t, 1:2],
            )

        aggregate(0)
        center(0)
        root(0)
        sum_up(1, 3)
        keep_awake(y_bank[1, 3][:, UNIT_ROWS:], idle_operand[:, 0:LATER_IDLE_COLS])
        aggregate(1)
        center(1)
        root(1)
        make_scale_shift(0)
        make_scale_shift(1)
        def normalise(n):
            parts = UNIT_TILES if n == 0 else 1
            width = UNIT_ROWS // parts
            for part in range(parts):
                rows = slice(part * width, (part + 1) * width)
                normalise_on_vector(0, n, rows)
                normalise_on_scalar(1, n, rows)

        for n in range(LEAD):
            normalise(n)

        for n in range(UNITS):
            if n + LEAD < UNITS:
                normalise(n + LEAD)
            result = keep.tile([P, UNIT_TILES, EMB], F32, name="result%d" % n)
            for i in range(UNIT_TILES):
                out_bank = banks.tile([P, EMB], F32, tag="bank", name="out_bank%d%d" % (n, i))
                for t in range(O_TILES):
                    nc.tensor.transpose(
                        out_bank[:, t * P : (t + 1) * P],
                        z[t, n][:, i * P : (i + 1) * P],
                        ident[:],
                    )
                source = out_bank[:].rearrange("p (t o) -> p o t", t=O_TILES)
                target = result[:, i, :].rearrange("p (o t) -> p o t", t=O_TILES)
                if i == 0:
                    nc.scalar.activation(out=target, in_=source, func=ACT.Relu)
                else:
                    nc.vector.tensor_scalar_max(out=target, in0=source, scalar1=0.0)
                if n == 0:
                    nc.sync.dma_start(out=out_rows[:, i, :], in_=result[:, i, :])
            if n > 0:
                nc.sync.dma_start(
                    out=out_rows[:, n * UNIT_TILES : (n + 1) * UNIT_TILES, :], in_=result[:]
                )
